import numpy as np
import ml_dtypes


def mxq(x, axis, fmt="e4m3"):
    dtype, down = {"e4m3": (ml_dtypes.float8_e4m3fn, 7), "e5m2": (ml_dtypes.float8_e5m2, 14)}[fmt]
    v = np.moveaxis(np.asarray(x, np.float32).astype(ml_dtypes.bfloat16).astype(np.float64), axis, -1)
    blocks = v.reshape(v.shape[:-1] + (-1, 32))
    amax = np.abs(blocks).max(-1, keepdims=True)
    byte = np.maximum(np.where(amax > 0, np.frexp(amax)[1] - 1 + 127, 0) - down, 1)
    scale = np.exp2(byte - 127.0)
    codes = (blocks / scale).astype(np.float32).astype(dtype).astype(np.float64)
    return np.moveaxis((codes * scale).reshape(v.shape), -1, axis)


WIDE = False


def mx_kscale(k):
    if not WIDE:
        return np.ones(k)
    levels = np.array([10, -10, 5, -5, 0])
    a = np.random.permutation(np.resize(levels, k // 512 * 4)).reshape(k // 512, 4)
    idx = np.arange(k)
    return np.exp2(a[idx // 512, idx % 128 // 32])


BF16 = ml_dtypes.bfloat16


def bf(x):
    return np.asarray(x, np.float32).astype(BF16)


def f64(x):
    return np.asarray(x).astype(np.float64)


B, L, D, NC, DS = 2, 64, 512, 2, 3
EPS = 2.0 ** -23


def rmsnorm(v, w):
    ms = np.mean(np.square(v), axis=-1, keepdims=True)
    return v * (1.0 / np.sqrt(ms + EPS)) * w


def setup_inputs():
    s = mx_kscale(D)
    s = s / s.max()
    t = mx_kscale(NC * D)
    tc = t.reshape(NC, D, 1)
    return {"x": bf(np.random.standard_normal((B, L, D)) * s),
            "W_in": bf(np.random.standard_normal((NC * D, D)) / np.sqrt(D) / s[None, :]),
            "W_out": bf(np.random.standard_normal((D, NC * D)) / np.sqrt(NC * D) / t[None, :]),
            "A_theta": bf(np.random.standard_normal((NC, D, DS)) * 0.5),
            "B_real": bf(np.random.standard_normal((NC, D, DS))),
            "B_imag": bf(np.random.standard_normal((NC, D, DS))),
            "C_real": bf(np.random.standard_normal((NC, D, DS)) / np.sqrt(2 * DS) * tc),
            "C_imag": bf(np.random.standard_normal((NC, D, DS)) / np.sqrt(2 * DS) * tc),
            "norm_w": bf(1.0 + 0.1 * np.random.standard_normal(D))}


def reference(x, W_in, W_out, A_theta, B_real, B_imag, C_real, C_imag, norm_w):
    x = f64(x)
    b, l, _ = x.shape
    xi = (mxq(x, 2, "e4m3") @ mxq(f64(W_in), 1, "e4m3").T).reshape(b, l, NC, D)[..., None]
    ct = np.cos(f64(A_theta))
    st = np.sin(f64(A_theta))
    rs = np.zeros((b, l, NC, D, DS))
    is_ = np.zeros_like(rs)
    bxr = f64(B_real) * xi
    bxi = f64(B_imag) * xi
    nr = ct * rs - st * is_ + bxr
    ni = st * rs + ct * is_ + bxi
    y = np.sum(f64(C_real) * nr - f64(C_imag) * ni, axis=-1)
    out = mxq(y.reshape(b, l, NC * D), 2, "e4m3") @ mxq(f64(W_out), 1, "e4m3").T
    return x + rmsnorm(out, f64(norm_w)), nr, ni

@@ -1,0 +1,306 @@
+from contextlib import ExitStack
+
+from concourse import mybir
+from concourse.masks import make_identity
+
+F32 = mybir.dt.float32
+BF16 = mybir.dt.bfloat16
+U32 = mybir.dt.uint32
+U8 = mybir.dt.uint8
+FP8X4 = mybir.dt.float8_e4m3fn_x4
+ALU = mybir.AluOpType
+ACT = mybir.ActivationFunctionType
+
+P = 128
+D = 512
+HALVES = 2
+CHUNKS = 4
+STATES = 3
+COLS = HALVES * D
+FLAT = COLS * STATES
+HALF_FLAT = FLAT // HALVES
+BANK = 512
+EPS = 2.0 ** -23
+
+FLOPS = 2 * (2 * P * D * COLS)
+
+
+def tile_mamba3core_s_kernel(
+    tc, x, W_in, W_out, A_theta, B_real, B_imag, C_real, C_imag, norm_w, out_0, out_1, out_2
+):
+    nc = tc.nc
+    x_rows = x.flatten_outer_dims()
+    res_rows = out_0.flatten_outer_dims()
+    state_rows = {
+        "r": out_1.rearrange("b l c d n -> (b l) (c d n)"),
+        "i": out_2.rearrange("b l c d n -> (b l) (c d n)"),
+    }
+
+    with ExitStack() as ctx:
+        keep = ctx.enter_context(tc.tile_pool(name="keep", bufs=1))
+        flips = ctx.enter_context(tc.psum_pool(name="flips", bufs=3))
+        xi_tok = ctx.enter_context(tc.psum_pool(name="xi_tok", bufs=2))
+        xi_col = ctx.enter_context(tc.psum_pool(name="xi_col", bufs=2))
+        out_acc = ctx.enter_context(tc.psum_pool(name="out_acc", bufs=1))
+
+        vec_rows = keep.tile([P, 2 * P], BF16)
+        nc.gpsimd.memset(vec_rows[:].bitcast(F32), 0.0)
+        ident = keep.tile([P, P], F32)
+        make_identity(nc, ident[:])
+        eps = keep.tile([P, 1], F32)
+        nc.vector.memset(eps[:], EPS)
+
+        b_rows = FLAT // (2 * P)
+        nc.sync.dma_start(
+            out=vec_rows[0:b_rows, :],
+            in_=B_real.rearrange("a d n -> (a d n)").rearrange("(r w) -> r w", w=2 * P),
+        )
+        nc.sync.dma_start(
+            out=vec_rows[b_rows : 2 * b_rows, :],
+            in_=B_imag.rearrange("a d n -> (a d n)").rearrange("(r w) -> r w", w=2 * P),
+        )
+        nc.sync.dma_start(
+            out=vec_rows[2 * b_rows : 2 * b_rows + 2, :],
+            in_=norm_w.rearrange("(r w) -> r w", w=2 * P),
+        )
+
+        x_sb = keep.tile([P, D], BF16)
+        nc.sync.dma_start(out=x_sb[:], in_=x_rows)
+        wi_sb = keep.tile([P, HALVES, CHUNKS * D], BF16)
+        for h in range(HALVES):
+            nc.sync.dma_start(
+                out=wi_sb[:, h, :],
+                in_=W_in[D * h : D * (h + 1), :].rearrange("(p c) k -> p (c k)", c=CHUNKS),
+            )
+        small = {}
+        for name, src in (("br", B_real), ("bi", B_imag), ("cr", C_real), ("ci", C_imag)):
+            small[name] = keep.tile([P, HALVES, CHUNKS * STATES], BF16, name="small_" + name)
+            nc.scalar.dma_start(
+                out=small[name][:], in_=src.rearrange("h (p c) n -> p h (c n)", c=CHUNKS)
+            )
+        warm = keep.tile([P, 1], F32)
+        nc.scalar.activation(out=warm[:], in_=eps[:], func=ACT.Sqrt)
+        wo_sb = keep.tile([P, 4, COLS], BF16)
+        for pair in range(2):
+            nc.sync.dma_start(
+                out=wo_sb[:, 2 * pair : 2 * pair + 2, :],
+                in_=W_out[256 * pair : 256 * (pair + 1), :].rearrange("(i q) k -> q i k", q=P),
+            )
+
+        bank = flips.tile([P, BANK], F32, tag="flip")
+        nc.tensor.transpose(bank[:, 0:P], vec_rows[:].bitcast(F32), ident[:])
+        vec_cols = keep.tile([P, 32], F32)
+        nc.scalar.copy(out=vec_cols[:], in_=bank[:, 0:32])
+
+        spread = {
+            "r": keep.tile([P, FLAT], BF16, name="spread_r"),
+            "i": keep.tile([P, FLAT], BF16, name="spread_i"),
+            "w": keep.tile([P, D], BF16, name="spread_w"),
+        }
+
+        def spread_rows(which, first_row, first_word, rows):
+            bank = flips.tile([P, BANK], F32, tag="flip")
+            for r in range(rows):
+                nc.tensor.transpose(
+                    bank[:, P * r : P * (r + 1)],
+                    vec_cols[:, first_row + r : first_row + r + 1].to_broadcast([P, P]),
+                    ident[:],
+                )
+            nc.scalar.copy(
+                out=spread[which][:].bitcast(F32)[:, first_word : first_word + P * rows],
+                in_=bank[:, 0 : P * rows],
+            )
+
+        spread_rows("r", 0, 0, 4)
+        spread_rows("r", 4, BANK, 4)
+
+        x_grouped = keep.tile([P, P * 4], BF16, align_bytes=64)
+        x_codes = keep.tile([P, P], U32, align_bytes=64)
+        x_scales = keep.tile([P, P], U8, align_bytes=64)
+        bank = flips.tile([P, BANK], F32, tag="flip")
+        for u in range(2):
+            nc.tensor.transpose(
+                bank[:, P * u : P * (u + 1)], x_sb[:].bitcast(F32)[:, P * u : P * (u + 1)], ident[:]
+            )
+        nc.vector.tensor_copy(
+            out=x_grouped[:].bitcast(F32).rearrange("w (t u) -> w t u", u=2),
+            in_=bank[:, 0 : 2 * P].rearrange("w (u t) -> w t u", u=2),
+        )
+        nc.vector.quantize_mx(out=x_codes[:].bitcast(FP8X4), scales=x_scales[:], in_=x_grouped[:])
+
+        wi_grouped = keep.tile([P, COLS * 4], BF16, align_bytes=64)
+        wi_codes = keep.tile([P, COLS], U32, align_bytes=64)
+        wi_scales = keep.tile([P, COLS], U8, align_bytes=64)
+
+        def flip_w_in(h):
+            for pair in range(2):
+                bank = flips.tile([P, BANK], F32, tag="flip")
+                for cl in range(2):
+                    for u in range(2):
+                        first = 256 * (2 * pair + cl) + P * u
+                        nc.tensor.transpose(
+                            bank[:, P * (2 * cl + u) : P * (2 * cl + u + 1)],
+                            wi_sb[:, h, :].bitcast(F32)[:, first : first + P],
+                            ident[:],
+                        )
+                words = 2 * (D * h + 256 * pair)
+                dst = wi_grouped[:].bitcast(F32)[:, words : words + BANK]
+                copy = nc.scalar.copy if pair == 0 else nc.vector.tensor_copy
+                copy(
+                    out=dst.rearrange("w (cl p u) -> w cl p u", cl=2, u=2),
+                    in_=bank[:].rearrange("w (cl u p) -> w cl p u", cl=2, u=2),
+                )
+            nc.vector.quantize_mx(
+                out=wi_codes[:, D * h : D * (h + 1)].bitcast(FP8X4),
+                scales=wi_scales[:, D * h : D * (h + 1)],
+                in_=wi_grouped[:, 4 * D * h : 4 * D * (h + 1)],
+            )
+
+        rr = keep.tile([P, HALVES * CHUNKS, STATES], F32)
+        ii = keep.tile([P, HALVES * CHUNKS, STATES], F32)
+        gain = keep.tile([P, HALVES, CHUNKS], F32)
+
+        def make_gain():
+            nc.vector.tensor_tensor(
+                out=rr[:].rearrange("p a n -> p (a n)"),
+                in0=small["cr"][:].rearrange("p h m -> p (h m)"),
+                in1=small["br"][:].rearrange("p h m -> p (h m)"),
+                op=ALU.mult,
+            )
+            nc.vector.tensor_tensor(
+                out=ii[:].rearrange("p a n -> p (a n)"),
+                in0=small["ci"][:].rearrange("p h m -> p (h m)"),
+                in1=small["bi"][:].rearrange("p h m -> p (h m)"),
+                op=ALU.mult,
+            )
+            nc.vector.tensor_tensor(out=rr[:], in0=rr[:], in1=ii[:], op=ALU.subtract)
+            nc.vector.tensor_reduce(
+                out=gain[:].rearrange("p h c -> p (h c)"), in_=rr[:], axis=mybir.AxisListType.X, op=ALU.add
+            )
+
+        state_sb = {
+            "r": keep.tile([P, FLAT], F32, name="state_r"),
+            "i": keep.tile([P, FLAT], F32, name="state_i"),
+        }
+        y_grouped = keep.tile([P, HALVES, P, CHUNKS], BF16, align_bytes=64)
+        xi_by_token = {}
+        xi_by_column = {}
+
+        def first_matmul(h):
+            xi_by_token[h] = xi_tok.tile([P, BANK], F32, name="xi_by_token", tag="xi_tok")
+            nc.tensor.matmul_mx(
+                out=xi_by_token[h][:],
+                lhsT=x_codes[:].bitcast(FP8X4),
+                lhsT_scale=x_scales[:],
+                rhs=wi_codes[:, D * h : D * (h + 1)].bitcast(FP8X4),
+                rhs_scale=wi_scales[:, D * h : D * (h + 1)],
+                start=True,
+                stop=True,
+            )
+            xi_by_column[h] = xi_col.tile([P, CHUNKS, P], F32, name="xi_by_column", tag="xi_col")
+            for c in range(CHUNKS):
+                cols = slice(D * h + P * c, D * h + P * (c + 1))
+                nc.tensor.matmul_mx(
+                    out=xi_by_column[h][:, c, :],
+                    lhsT=wi_codes[:, cols].bitcast(FP8X4),
+                    lhsT_scale=wi_scales[:, cols],
+                    rhs=x_codes[:].bitcast(FP8X4),
+                    rhs_scale=x_scales[:],
+                    start=True,
+                    stop=True,
+                )
+
+        def states(which, h):
+            cols = slice(HALF_FLAT * h, HALF_FLAT * (h + 1))
+            nc.vector.tensor_tensor(
+                out=state_sb[which][:, cols].rearrange("t (p c n) -> t p c n", c=CHUNKS, n=STATES),
+                in0=xi_by_token[h][:]
+                .rearrange("t (c p) -> t p c", c=CHUNKS)
+                .unsqueeze(3)
+                .to_broadcast([P, P, CHUNKS, STATES]),
+                in1=spread[which][:, cols].rearrange("t (p c n) -> t p c n", c=CHUNKS, n=STATES),
+                op=ALU.mult,
+            )
+            nc.sync.dma_start(out=state_rows[which][:, cols], in_=state_sb[which][:, cols])
+
+        def make_y(h):
+            nc.vector.tensor_tensor(
+                out=y_grouped[:, h, :, :],
+                in0=xi_by_column[h][:].rearrange("p c t -> p t c"),
+                in1=gain[:, h, :].unsqueeze(1).to_broadcast([P, P, CHUNKS]),
+                op=ALU.mult,
+            )
+
+        flip_w_in(0)
+        spread_rows("i", 12, 0, 4)
+        spread_rows("i", 16, BANK, 4)
+        first_matmul(0)
+        make_gain()
+        states("r", 0)
+        flip_w_in(1)
+        spread_rows("r", 8, 2 * BANK, 4)
+        spread_rows("i", 20, 2 * BANK, 4)
+        first_matmul(1)
+        states("i", 0)
+        make_y(0)
+        make_y(1)
+        y_codes = keep.tile([P, HALVES * P], U32, align_bytes=64)
+        y_scales = keep.tile([P, HALVES * P], U8, align_bytes=64)
+        nc.vector.quantize_mx(
+            out=y_codes[:].bitcast(FP8X4),
+            scales=y_scales[:],
+            in_=y_grouped[:].rearrange("p h t c -> p (h t c)"),
+        )
+        states("r", 1)
+
+        spread_rows("w", 24, 0, 2)
+        wo_grouped = keep.tile([P, HALVES, D * 4], BF16, align_bytes=64)
+        wo_codes = keep.tile([P, HALVES, D], U32, align_bytes=64)
+        wo_scales = keep.tile([P, HALVES, D], U8, align_bytes=64)
+        for pair in range(2):
+            for h in range(HALVES):
+                bank = flips.tile([P, BANK], F32, tag="flip")
+                for il in range(2):
+                    for u in range(2):
+                        nc.tensor.transpose(
+                            bank[:, P * (2 * il + u) : P * (2 * il + u + 1)],
+                            wo_sb[:, 2 * pair + il, :].bitcast(F32)[:, 256 * h + u : 256 * (h + 1) : 2],
+                            ident[:],
+                        )
+                dst = wo_grouped[:, h, :].bitcast(F32)[:, BANK * pair : BANK * (pair + 1)]
+                nc.scalar.copy(
+                    out=dst.rearrange("p (il q u) -> p il q u", il=2, u=2),
+                    in_=bank[:].rearrange("p (il u q) -> p il q u", il=2, u=2),
+                )
+        for h in range(HALVES):
+            nc.vector.quantize_mx(
+                out=wo_codes[:, h, :].bitcast(FP8X4), scales=wo_scales[:, h, :], in_=wo_grouped[:, h, :]
+            )
+
+        acc = out_acc.tile([P, D], F32)
+        for h in range(HALVES):
+            nc.tensor.matmul_mx(
+                out=acc[:],
+                lhsT=y_codes[:, P * h : P * (h + 1)].bitcast(FP8X4),
+                lhsT_scale=y_scales[:, P * h : P * (h + 1)],
+                rhs=wo_codes[:, h, :].bitcast(FP8X4),
+                rhs_scale=wo_scales[:, h, :],
+                start=(h == 0),
+                stop=(h == HALVES - 1),
+            )
+
+        squares = keep.tile([P, D], F32)
+        sum_sq = keep.tile([P, 1], F32)
+        nc.scalar.activation(out=squares[:], in_=acc[:], func=ACT.Square, accum_out=sum_sq[:])
+        rms = keep.tile([P, 1], F32)
+        nc.scalar.activation(out=rms[:], in_=sum_sq[:], func=ACT.Sqrt, bias=eps[:], scale=1.0 / D)
+        inv_rms = keep.tile([P, 1], F32)
+        nc.vector.reciprocal(out=inv_rms[:], in_=rms[:])
+        res = keep.tile([P, D], F32)
+        nc.vector.scalar_tensor_tensor(
+            out=res[:], in0=acc[:], scalar=inv_rms[:], in1=spread["w"][:], op0=ALU.mult, op1=ALU.mult
+        )
+        nc.vector.tensor_tensor(out=res[:], in0=res[:], in1=x_sb[:], op=ALU.add)
+        nc.sync.dma_start(out=res_rows, in_=res[:])
+
+        states("i", 1)

@@ -13,14 +13,17 @@ ACT = mybir.ActivationFunctionType
 
 P = 128
 D = 512
-HALVES = 2
-CHUNKS = 4
+PASSES = 2
+GROUPS = 4
+GROUP_COLS = 2 * P
 STATES = 3
-COLS = HALVES * D
-FLAT = COLS * STATES
-HALF_FLAT = FLAT // HALVES
+COLS = GROUPS * GROUP_COLS
+GROUP_FLAT = GROUP_COLS * STATES
+GROUP_WORDS = GROUP_FLAT // 2
+FLAT = GROUPS * GROUP_FLAT
 BANK = 512
 EPS = 2.0 ** -23
+GPSIMD_GROUPS = 3
 
 FLOPS = 2 * (2 * P * D * COLS)
 
@@ -43,54 +46,76 @@ def tile_mamba3core_s_kernel(
         xi_col = ctx.enter_context(tc.psum_pool(name="xi_col", bufs=2))
         out_acc = ctx.enter_context(tc.psum_pool(name="out_acc", bufs=1))
 
-        vec_rows = keep.tile([P, 2 * P], BF16)
+        vec_rows = keep.tile([P, GROUP_FLAT], BF16)
         nc.gpsimd.memset(vec_rows[:].bitcast(F32), 0.0)
         ident = keep.tile([P, P], F32)
         make_identity(nc, ident[:])
         eps = keep.tile([P, 1], F32)
         nc.vector.memset(eps[:], EPS)
 
-        b_rows = FLAT // (2 * P)
+        for v, src in enumerate((B_real, B_imag, C_real, C_imag)):
+            nc.sync.dma_start(
+                out=vec_rows[GROUPS * v : GROUPS * (v + 1), :],
+                in_=src.rearrange("a d n -> (a d n)").rearrange("(g f) -> g f", f=GROUP_FLAT),
+            )
+        NORM_ROW = 4 * GROUPS
         nc.sync.dma_start(
-            out=vec_rows[0:b_rows, :],
-            in_=B_real.rearrange("a d n -> (a d n)").rearrange("(r w) -> r w", w=2 * P),
+            out=vec_rows[NORM_ROW : NORM_ROW + 1, 0:D], in_=norm_w.rearrange("(o d) -> o d", o=1)
         )
-        nc.sync.dma_start(
-            out=vec_rows[b_rows : 2 * b_rows, :],
-            in_=B_imag.rearrange("a d n -> (a d n)").rearrange("(r w) -> r w", w=2 * P),
-        )
-        nc.sync.dma_start(
-            out=vec_rows[2 * b_rows : 2 * b_rows + 2, :],
-            in_=norm_w.rearrange("(r w) -> r w", w=2 * P),
-        )
-
         x_sb = keep.tile([P, D], BF16)
         nc.sync.dma_start(out=x_sb[:], in_=x_rows)
-        wi_sb = keep.tile([P, HALVES, CHUNKS * D], BF16)
-        for h in range(HALVES):
+        wi_sb = keep.tile([P, GROUPS, 2 * D], BF16)
+        for g in range(GROUPS):
             nc.sync.dma_start(
-                out=wi_sb[:, h, :],
-                in_=W_in[D * h : D * (h + 1), :].rearrange("(p c) k -> p (c k)", c=CHUNKS),
+                out=wi_sb[:, g, :],
+                in_=W_in[GROUP_COLS * g : GROUP_COLS * (g + 1), :].rearrange("(p e) k -> p (e k)", e=2),
             )
-        small = {}
-        for name, src in (("br", B_real), ("bi", B_imag), ("cr", C_real), ("ci", C_imag)):
-            small[name] = keep.tile([P, HALVES, CHUNKS * STATES], BF16, name="small_" + name)
-            nc.scalar.dma_start(
-                out=small[name][:], in_=src.rearrange("h (p c) n -> p h (c n)", c=CHUNKS)
-            )
-        warm = keep.tile([P, 1], F32)
-        nc.scalar.activation(out=warm[:], in_=eps[:], func=ACT.Sqrt)
         wo_sb = keep.tile([P, 4, COLS], BF16)
         for pair in range(2):
             nc.sync.dma_start(
                 out=wo_sb[:, 2 * pair : 2 * pair + 2, :],
                 in_=W_out[256 * pair : 256 * (pair + 1), :].rearrange("(i q) k -> q i k", q=P),
             )
+        warm = keep.tile([P, 1], F32)
+        nc.scalar.activation(out=warm[:], in_=eps[:], func=ACT.Sqrt)
 
+        vec_words = vec_rows[:].bitcast(F32)
         bank = flips.tile([P, BANK], F32, tag="flip")
-        nc.tensor.transpose(bank[:, 0:P], vec_rows[:].bitcast(F32), ident[:])
-        vec_cols = keep.tile([P, 32], F32)
-        nc.scalar.copy(out=vec_cols[:], in_=bank[:, 0:32])
+        for s in range(3):
+            nc.tensor.transpose(bank[:, P * s : P * (s + 1)], vec_words[:, P * s : P * (s + 1)], ident[:])
+        vec_cols = keep.tile([P, 3, 32], F32)
+        nc.scalar.copy(
+            out=vec_cols[:], in_=bank[:, 0 : 3 * P].rearrange("w (s r) -> w s r", s=3)[:, :, 0:32]
+        )
+        bank = flips.tile([P, BANK], F32, tag="flip")
+        for s in range(3):
+            nc.tensor.transpose(bank[:, P * s : P * (s + 1)], vec_words[:, s : GROUP_WORDS : 3], ident[:])
+        own_words = keep.tile([P, 4 * GROUPS, 3], F32)
+        nc.vector.tensor_copy(
+            out=own_words[:], in_=bank[:, 0 : 3 * P].rearrange("p (s r) -> p r s", s=3)[:, 0 : 4 * GROUPS, :]
+        )
+        own = own_words[:].rearrange("p r s -> p (r s)").bitcast(BF16)
+        per_vec = GROUPS * 2 * STATES
+
+        rr = keep.tile([P, GROUPS * 2, STATES], F32)
+        ii = keep.tile([P, GROUPS * 2, STATES], F32)
+        gain = keep.tile([P, PASSES, 4], F32)
+        nc.vector.tensor_tensor(
+            out=rr[:].rearrange("p a n -> p (a n)"),
+            in0=own[:, 2 * per_vec : 3 * per_vec],
+            in1=own[:, 0:per_vec],
+            op=ALU.mult,
+        )
+        nc.vector.tensor_tensor(
+            out=ii[:].rearrange("p a n -> p (a n)"),
+            in0=own[:, 3 * per_vec : 4 * per_vec],
+            in1=own[:, per_vec : 2 * per_vec],
+            op=ALU.mult,
+        )
+        nc.vector.tensor_tensor(out=rr[:], in0=rr[:], in1=ii[:], op=ALU.subtract)
+        nc.vector.tensor_reduce(
+            out=gain[:].rearrange("p h j -> p (h j)"), in_=rr[:], axis=mybir.AxisListType.X, op=ALU.add
+        )
 
         spread = {
             "r": keep.tile([P, FLAT], BF16, name="spread_r"),
@@ -98,21 +123,24 @@ def tile_mamba3core_s_kernel(
             "w": keep.tile([P, D], BF16, name="spread_w"),
         }
 
-        def spread_rows(which, first_row, first_word, rows):
+        def spread_row(which, row, first_word, slices):
             bank = flips.tile([P, BANK], F32, tag="flip")
-            for r in range(rows):
+            for s in range(slices):
                 nc.tensor.transpose(
-                    bank[:, P * r : P * (r + 1)],
-                    vec_cols[:, first_row + r : first_row + r + 1].to_broadcast([P, P]),
+                    bank[:, P * s : P * (s + 1)],
+                    vec_cols[:, s, row : row + 1].to_broadcast([P, P]),
                     ident[:],
                 )
             nc.scalar.copy(
-                out=spread[which][:].bitcast(F32)[:, first_word : first_word + P * rows],
-                in_=bank[:, 0 : P * rows],
+                out=spread[which][:].bitcast(F32)[:, first_word : first_word + P * slices],
+                in_=bank[:, 0 : P * slices],
             )
 
-        spread_rows("r", 0, 0, 4)
-        spread_rows("r", 4, BANK, 4)
+        def spread_group(g):
+            spread_row("r", g, GROUP_WORDS * g, 3)
+            spread_row("i", GROUPS + g, GROUP_WORDS * g, 3)
+
+        spread_group(0)
 
         x_grouped = keep.tile([P, P * 4], BF16, align_bytes=64)
         x_codes = keep.tile([P, P], U32, align_bytes=64)
@@ -132,153 +160,155 @@ def tile_mamba3core_s_kernel(
         wi_codes = keep.tile([P, COLS], U32, align_bytes=64)
         wi_scales = keep.tile([P, COLS], U8, align_bytes=64)
 
-        def flip_w_in(h):
-            for pair in range(2):
-                bank = flips.tile([P, BANK], F32, tag="flip")
-                for cl in range(2):
-                    for u in range(2):
-                        first = 256 * (2 * pair + cl) + P * u
-                        nc.tensor.transpose(
-                            bank[:, P * (2 * cl + u) : P * (2 * cl + u + 1)],
-                            wi_sb[:, h, :].bitcast(F32)[:, first : first + P],
-                            ident[:],
-                        )
-                words = 2 * (D * h + 256 * pair)
-                dst = wi_grouped[:].bitcast(F32)[:, words : words + BANK]
-                copy = nc.scalar.copy if pair == 0 else nc.vector.tensor_copy
-                copy(
-                    out=dst.rearrange("w (cl p u) -> w cl p u", cl=2, u=2),
-                    in_=bank[:].rearrange("w (cl u p) -> w cl p u", cl=2, u=2),
-                )
+        def flip_w_in(g):
+            cols = slice(GROUP_COLS * g, GROUP_COLS * (g + 1))
+            bank = flips.tile([P, BANK], F32, tag="flip")
+            for e in range(2):
+                for u in range(2):
+                    first = 256 * e + P * u
+                    nc.tensor.transpose(
+                        bank[:, P * (2 * e + u) : P * (2 * e + u + 1)],
+                        wi_sb[:, g, :].bitcast(F32)[:, first : first + P],
+                        ident[:],
+                    )
+            copy = nc.vector.tensor_copy if g == 0 else nc.scalar.copy
+            copy(
+                out=wi_grouped[:].bitcast(F32)[:, BANK * g : BANK * (g + 1)].rearrange(
+                    "w (e p u) -> w e p u", e=2, u=2
+                ),
+                in_=bank[:].rearrange("w (e u p) -> w e p u", e=2, u=2),
+            )
             nc.vector.quantize_mx(
-                out=wi_codes[:, D * h : D * (h + 1)].bitcast(FP8X4),
-                scales=wi_scales[:, D * h : D * (h + 1)],
-                in_=wi_grouped[:, 4 * D * h : 4 * D * (h + 1)],
-            )
-
-        rr = keep.tile([P, HALVES * CHUNKS, STATES], F32)
-        ii = keep.tile([P, HALVES * CHUNKS, STATES], F32)
-        gain = keep.tile([P, HALVES, CHUNKS], F32)
-
-        def make_gain():
-            nc.vector.tensor_tensor(
-                out=rr[:].rearrange("p a n -> p (a n)"),
-                in0=small["cr"][:].rearrange("p h m -> p (h m)"),
-                in1=small["br"][:].rearrange("p h m -> p (h m)"),
-                op=ALU.mult,
-            )
-            nc.vector.tensor_tensor(
-                out=ii[:].rearrange("p a n -> p (a n)"),
-                in0=small["ci"][:].rearrange("p h m -> p (h m)"),
-                in1=small["bi"][:].rearrange("p h m -> p (h m)"),
-                op=ALU.mult,
-            )
-            nc.vector.tensor_tensor(out=rr[:], in0=rr[:], in1=ii[:], op=ALU.subtract)
-            nc.vector.tensor_reduce(
-                out=gain[:].rearrange("p h c -> p (h c)"), in_=rr[:], axis=mybir.AxisListType.X, op=ALU.add
+                out=wi_codes[:, cols].bitcast(FP8X4),
+                scales=wi_scales[:, cols],
+                in_=wi_grouped[:, 4 * GROUP_COLS * g : 4 * GROUP_COLS * (g + 1)],
             )
 
         state_sb = {
             "r": keep.tile([P, FLAT], F32, name="state_r"),
             "i": keep.tile([P, FLAT], F32, name="state_i"),
         }
-        y_grouped = keep.tile([P, HALVES, P, CHUNKS], BF16, align_bytes=64)
+        xi_sb = keep.tile([P, COLS], F32)
+        y_grouped = keep.tile([P, PASSES, P, 4], BF16, align_bytes=64)
         xi_by_token = {}
         xi_by_column = {}
 
-        def first_matmul(h):
-            xi_by_token[h] = xi_tok.tile([P, BANK], F32, name="xi_by_token", tag="xi_tok")
+        def first_matmul(g):
+            h, half = divmod(g, 2)
+            cols = slice(GROUP_COLS * g, GROUP_COLS * (g + 1))
+            if half == 0:
+                xi_by_token[h] = xi_tok.tile([P, 2, GROUP_COLS], F32, name="xi_by_token", tag="xi_tok")
+                xi_by_column[h] = xi_col.tile([P, 4, P], F32, name="xi_by_column", tag="xi_col")
             nc.tensor.matmul_mx(
-                out=xi_by_token[h][:],
+                out=xi_by_token[h][:, half, :],
                 lhsT=x_codes[:].bitcast(FP8X4),
                 lhsT_scale=x_scales[:],
-                rhs=wi_codes[:, D * h : D * (h + 1)].bitcast(FP8X4),
-                rhs_scale=wi_scales[:, D * h : D * (h + 1)],
+                rhs=wi_codes[:, cols].bitcast(FP8X4),
+                rhs_scale=wi_scales[:, cols],
                 start=True,
                 stop=True,
             )
-            xi_by_column[h] = xi_col.tile([P, CHUNKS, P], F32, name="xi_by_column", tag="xi_col")
-            for c in range(CHUNKS):
-                cols = slice(D * h + P * c, D * h + P * (c + 1))
+            for e in range(2):
+                part = slice(GROUP_COLS * g + P * e, GROUP_COLS * g + P * (e + 1))
                 nc.tensor.matmul_mx(
-                    out=xi_by_column[h][:, c, :],
-                    lhsT=wi_codes[:, cols].bitcast(FP8X4),
-                    lhsT_scale=wi_scales[:, cols],
+                    out=xi_by_column[h][:, 2 * half + e, :],
+                    lhsT=wi_codes[:, part].bitcast(FP8X4),
+                    lhsT_scale=wi_scales[:, part],
                     rhs=x_codes[:].bitcast(FP8X4),
                     rhs_scale=x_scales[:],
                     start=True,
                     stop=True,
                 )
 
-        def states(which, h):
-            cols = slice(HALF_FLAT * h, HALF_FLAT * (h + 1))
-            nc.vector.tensor_tensor(
-                out=state_sb[which][:, cols].rearrange("t (p c n) -> t p c n", c=CHUNKS, n=STATES),
-                in0=xi_by_token[h][:]
-                .rearrange("t (c p) -> t p c", c=CHUNKS)
-                .unsqueeze(3)
-                .to_broadcast([P, P, CHUNKS, STATES]),
-                in1=spread[which][:, cols].rearrange("t (p c n) -> t p c n", c=CHUNKS, n=STATES),
-                op=ALU.mult,
-            )
-            nc.sync.dma_start(out=state_rows[which][:, cols], in_=state_sb[which][:, cols])
+        def states(which, g):
+            h, half = divmod(g, 2)
+            flat = slice(GROUP_FLAT * g, GROUP_FLAT * (g + 1))
+            in_order = xi_by_token[h][:, half, :].rearrange("t (e p) -> t p e", e=2)
+            if which == "i" and g < GPSIMD_GROUPS:
+                cols = slice(GROUP_COLS * g, GROUP_COLS * (g + 1))
+                nc.scalar.copy(out=xi_sb[:, cols].rearrange("t (p e) -> t p e", e=2), in_=in_order)
+                nc.gpsimd.tensor_tensor(
+                    out=state_sb[which][:, flat].rearrange("t (c n) -> t c n", n=STATES),
+                    in0=xi_sb[:, cols].unsqueeze(2).to_broadcast([P, GROUP_COLS, STATES]),
+                    in1=spread[which][:, flat].rearrange("t (c n) -> t c n", n=STATES),
+                    op=ALU.mult,
+                )
+            else:
+                nc.vector.tensor_tensor(
+                    out=state_sb[which][:, flat].rearrange("t (p e n) -> t p e n", e=2, n=STATES),
+                    in0=in_order.unsqueeze(3).to_broadcast([P, P, 2, STATES]),
+                    in1=spread[which][:, flat].rearrange("t (p e n) -> t p e n", e=2, n=STATES),
+                    op=ALU.mult,
+                )
+            nc.sync.dma_start(out=state_rows[which][:, flat], in_=state_sb[which][:, flat])
 
         def make_y(h):
             nc.vector.tensor_tensor(
                 out=y_grouped[:, h, :, :],
-                in0=xi_by_column[h][:].rearrange("p c t -> p t c"),
-                in1=gain[:, h, :].unsqueeze(1).to_broadcast([P, P, CHUNKS]),
+                in0=xi_by_column[h][:].rearrange("p j t -> p t j"),
+                in1=gain[:, h, :].unsqueeze(1).to_broadcast([P, P, 4]),
                 op=ALU.mult,
             )
 
+        wo_grouped = keep.tile([P, PASSES, D * 4], BF16, align_bytes=64)
+        wo_codes = keep.tile([P, PASSES, D], U32, align_bytes=64)
+        wo_scales = keep.tile([P, PASSES, D], U8, align_bytes=64)
+
+        def flip_w_out(pair):
+            for h in range(PASSES):
+                bank = flips.tile([P, BANK], F32, tag="flip")
+                for il in range(2):
+                    for a in range(2):
+                        first = 256 * h + P * a
+                        nc.tensor.transpose(
+                            bank[:, P * (2 * il + a) : P * (2 * il + a + 1)],
+                            wo_sb[:, 2 * pair + il, :].bitcast(F32)[:, first : first + P],
+                            ident[:],
+                        )
+                nc.scalar.copy(
+                    out=wo_grouped[:, h, :].bitcast(F32)[:, BANK * pair : BANK * (pair + 1)].rearrange(
+                        "p (il q a) -> p il q a", il=2, a=2
+                    ),
+                    in_=bank[:].rearrange("p (il a q) -> p il q a", il=2, a=2),
+                )
+
         flip_w_in(0)
-        spread_rows("i", 12, 0, 4)
-        spread_rows("i", 16, BANK, 4)
         first_matmul(0)
-        make_gain()
         states("r", 0)
-        flip_w_in(1)
-        spread_rows("r", 8, 2 * BANK, 4)
-        spread_rows("i", 20, 2 * BANK, 4)
-        first_matmul(1)
         states("i", 0)
+        spread_group(1)
+        flip_w_in(1)
+        first_matmul(1)
         make_y(0)
+        states("r", 1)
+        states("i", 1)
+        spread_group(2)
+        flip_w_in(2)
+        first_matmul(2)
+        states("r", 2)
+        states("i", 2)
+        spread_group(3)
+        flip_w_in(3)
+        first_matmul(3)
         make_y(1)
-        y_codes = keep.tile([P, HALVES * P], U32, align_bytes=64)
-        y_scales = keep.tile([P, HALVES * P], U8, align_bytes=64)
+        y_codes = keep.tile([P, PASSES * P], U32, align_bytes=64)
+        y_scales = keep.tile([P, PASSES * P], U8, align_bytes=64)
         nc.vector.quantize_mx(
             out=y_codes[:].bitcast(FP8X4),
             scales=y_scales[:],
-            in_=y_grouped[:].rearrange("p h t c -> p (h t c)"),
+            in_=y_grouped[:].rearrange("p h t j -> p (h t j)"),
         )
-        states("r", 1)
-
-        spread_rows("w", 24, 0, 2)
-        wo_grouped = keep.tile([P, HALVES, D * 4], BF16, align_bytes=64)
-        wo_codes = keep.tile([P, HALVES, D], U32, align_bytes=64)
-        wo_scales = keep.tile([P, HALVES, D], U8, align_bytes=64)
-        for pair in range(2):
-            for h in range(HALVES):
-                bank = flips.tile([P, BANK], F32, tag="flip")
-                for il in range(2):
-                    for u in range(2):
-                        nc.tensor.transpose(
-                            bank[:, P * (2 * il + u) : P * (2 * il + u + 1)],
-                            wo_sb[:, 2 * pair + il, :].bitcast(F32)[:, 256 * h + u : 256 * (h + 1) : 2],
-                            ident[:],
-                        )
-                dst = wo_grouped[:, h, :].bitcast(F32)[:, BANK * pair : BANK * (pair + 1)]
-                nc.scalar.copy(
-                    out=dst.rearrange("p (il q u) -> p il q u", il=2, u=2),
-                    in_=bank[:].rearrange("p (il u q) -> p il q u", il=2, u=2),
-                )
-        for h in range(HALVES):
+        flip_w_out(0)
+        flip_w_out(1)
+        spread_row("w", NORM_ROW, 0, 2)
+        for h in range(PASSES):
             nc.vector.quantize_mx(
                 out=wo_codes[:, h, :].bitcast(FP8X4), scales=wo_scales[:, h, :], in_=wo_grouped[:, h, :]
             )
+        states("r", 3)
 
         acc = out_acc.tile([P, D], F32)
-        for h in range(HALVES):
+        for h in range(PASSES):
             nc.tensor.matmul_mx(
                 out=acc[:],
                 lhsT=y_codes[:, P * h : P * (h + 1)].bitcast(FP8X4),
@@ -286,7 +316,7 @@ def tile_mamba3core_s_kernel(
                 rhs=wo_codes[:, h, :].bitcast(FP8X4),
                 rhs_scale=wo_scales[:, h, :],
                 start=(h == 0),
-                stop=(h == HALVES - 1),
+                stop=(h == PASSES - 1),
             )
 
         squares = keep.tile([P, D], F32)
@@ -303,4 +333,4 @@ def tile_mamba3core_s_kernel(
         nc.vector.tensor_tensor(out=res[:], in0=res[:], in1=x_sb[:], op=ALU.add)
         nc.sync.dma_start(out=res_rows, in_=res[:])
 
-        states("i", 1)
+        states("i", 3)

@@ -22,8 +22,8 @@ GROUP_FLAT = GROUP_COLS * STATES
 GROUP_WORDS = GROUP_FLAT // 2
 FLAT = GROUPS * GROUP_FLAT
 BANK = 512
+NORM_ROW = 4 * GROUPS
 EPS = 2.0 ** -23
-GPSIMD_GROUPS = 3
 
 FLOPS = 2 * (2 * P * D * COLS)
 
@@ -41,10 +41,10 @@ def tile_mamba3core_s_kernel(
 
     with ExitStack() as ctx:
         keep = ctx.enter_context(tc.tile_pool(name="keep", bufs=1))
-        flips = ctx.enter_context(tc.psum_pool(name="flips", bufs=3))
+        flips = ctx.enter_context(tc.psum_pool(name="flips", bufs=4))
         xi_tok = ctx.enter_context(tc.psum_pool(name="xi_tok", bufs=2))
         xi_col = ctx.enter_context(tc.psum_pool(name="xi_col", bufs=2))
-        out_acc = ctx.enter_context(tc.psum_pool(name="out_acc", bufs=1))
+        ctx.enter_context(tc.manual_schedule())
 
         vec_rows = keep.tile([P, GROUP_FLAT], BF16)
         nc.gpsimd.memset(vec_rows[:].bitcast(F32), 0.0)
@@ -58,7 +58,6 @@ def tile_mamba3core_s_kernel(
                 out=vec_rows[GROUPS * v : GROUPS * (v + 1), :],
                 in_=src.rearrange("a d n -> (a d n)").rearrange("(g f) -> g f", f=GROUP_FLAT),
             )
-        NORM_ROW = 4 * GROUPS
         nc.sync.dma_start(
             out=vec_rows[NORM_ROW : NORM_ROW + 1, 0:D], in_=norm_w.rearrange("(o d) -> o d", o=1)
         )
@@ -80,50 +79,52 @@ def tile_mamba3core_s_kernel(
         nc.scalar.activation(out=warm[:], in_=eps[:], func=ACT.Sqrt)
 
         vec_words = vec_rows[:].bitcast(F32)
-        bank = flips.tile([P, BANK], F32, tag="flip")
-        for s in range(3):
-            nc.tensor.transpose(bank[:, P * s : P * (s + 1)], vec_words[:, P * s : P * (s + 1)], ident[:])
         vec_cols = keep.tile([P, 3, 32], F32)
-        nc.scalar.copy(
-            out=vec_cols[:], in_=bank[:, 0 : 3 * P].rearrange("w (s r) -> w s r", s=3)[:, :, 0:32]
-        )
-        bank = flips.tile([P, BANK], F32, tag="flip")
-        for s in range(3):
-            nc.tensor.transpose(bank[:, P * s : P * (s + 1)], vec_words[:, s : GROUP_WORDS : 3], ident[:])
         own_words = keep.tile([P, 4 * GROUPS, 3], F32)
-        nc.vector.tensor_copy(
-            out=own_words[:], in_=bank[:, 0 : 3 * P].rearrange("p (s r) -> p r s", s=3)[:, 0 : 4 * GROUPS, :]
-        )
-        own = own_words[:].rearrange("p r s -> p (r s)").bitcast(BF16)
-        per_vec = GROUPS * 2 * STATES
-
         rr = keep.tile([P, GROUPS * 2, STATES], F32)
         ii = keep.tile([P, GROUPS * 2, STATES], F32)
         gain = keep.tile([P, PASSES, 4], F32)
-        nc.vector.tensor_tensor(
-            out=rr[:].rearrange("p a n -> p (a n)"),
-            in0=own[:, 2 * per_vec : 3 * per_vec],
-            in1=own[:, 0:per_vec],
-            op=ALU.mult,
-        )
-        nc.vector.tensor_tensor(
-            out=ii[:].rearrange("p a n -> p (a n)"),
-            in0=own[:, 3 * per_vec : 4 * per_vec],
-            in1=own[:, per_vec : 2 * per_vec],
-            op=ALU.mult,
-        )
-        nc.vector.tensor_tensor(out=rr[:], in0=rr[:], in1=ii[:], op=ALU.subtract)
-        nc.vector.tensor_reduce(
-            out=gain[:].rearrange("p h j -> p (h j)"), in_=rr[:], axis=mybir.AxisListType.X, op=ALU.add
-        )
 
-        spread = {
-            "r": keep.tile([P, FLAT], BF16, name="spread_r"),
-            "i": keep.tile([P, FLAT], BF16, name="spread_i"),
-            "w": keep.tile([P, D], BF16, name="spread_w"),
-        }
+        def turn_for_spreading():
+            bank = flips.tile([P, BANK], F32, tag="flip")
+            for s in range(3):
+                nc.tensor.transpose(
+                    bank[:, P * s : P * (s + 1)], vec_words[:, P * s : P * (s + 1)], ident[:]
+                )
+            nc.scalar.copy(
+                out=vec_cols[:], in_=bank[:, 0 : 3 * P].rearrange("w (s r) -> w s r", s=3)[:, :, 0:32]
+            )
 
-        def spread_row(which, row, first_word, slices):
+        def make_gain():
+            bank = flips.tile([P, BANK], F32, tag="flip")
+            for s in range(3):
+                nc.tensor.transpose(
+                    bank[:, P * s : P * (s + 1)], vec_words[:, s : GROUP_WORDS : 3], ident[:]
+                )
+            nc.vector.tensor_copy(
+                out=own_words[:],
+                in_=bank[:, 0 : 3 * P].rearrange("p (s r) -> p r s", s=3)[:, 0 : 4 * GROUPS, :],
+            )
+            own = own_words[:].rearrange("p r s -> p (r s)").bitcast(BF16)
+            per_vec = GROUPS * 2 * STATES
+            nc.vector.tensor_tensor(
+                out=rr[:].rearrange("p a n -> p (a n)"),
+                in0=own[:, 2 * per_vec : 3 * per_vec],
+                in1=own[:, 0:per_vec],
+                op=ALU.mult,
+            )
+            nc.vector.tensor_tensor(
+                out=ii[:].rearrange("p a n -> p (a n)"),
+                in0=own[:, 3 * per_vec : 4 * per_vec],
+                in1=own[:, per_vec : 2 * per_vec],
+                op=ALU.mult,
+            )
+            nc.vector.tensor_tensor(out=rr[:], in0=rr[:], in1=ii[:], op=ALU.subtract)
+            nc.vector.tensor_reduce(
+                out=gain[:].rearrange("p h j -> p (h j)"), in_=rr[:], axis=mybir.AxisListType.X, op=ALU.add
+            )
+
+        def spread_row(row, slices):
             bank = flips.tile([P, BANK], F32, tag="flip")
             for s in range(slices):
                 nc.tensor.transpose(
@@ -131,30 +132,37 @@ def tile_mamba3core_s_kernel(
                     vec_cols[:, s, row : row + 1].to_broadcast([P, P]),
                     ident[:],
                 )
+            return bank
+
+        b_imag_all = keep.tile([P, FLAT], BF16)
+        norm_w_all = keep.tile([P, D], BF16)
+
+        def spread_b_imag(g):
+            bank = spread_row(GROUPS + g, 3)
             nc.scalar.copy(
-                out=spread[which][:].bitcast(F32)[:, first_word : first_word + P * slices],
-                in_=bank[:, 0 : P * slices],
+                out=b_imag_all[:].bitcast(F32)[:, GROUP_WORDS * g : GROUP_WORDS * (g + 1)],
+                in_=bank[:, 0:GROUP_WORDS],
             )
 
-        def spread_group(g):
-            spread_row("r", g, GROUP_WORDS * g, 3)
-            spread_row("i", GROUPS + g, GROUP_WORDS * g, 3)
-
-        spread_group(0)
+        def spread_norm_w():
+            bank = spread_row(NORM_ROW, 2)
+            nc.scalar.copy(out=norm_w_all[:].bitcast(F32), in_=bank[:, 0 : D // 2])
 
         x_grouped = keep.tile([P, P * 4], BF16, align_bytes=64)
         x_codes = keep.tile([P, P], U32, align_bytes=64)
         x_scales = keep.tile([P, P], U8, align_bytes=64)
-        bank = flips.tile([P, BANK], F32, tag="flip")
-        for u in range(2):
-            nc.tensor.transpose(
-                bank[:, P * u : P * (u + 1)], x_sb[:].bitcast(F32)[:, P * u : P * (u + 1)], ident[:]
+
+        def flip_x():
+            bank = flips.tile([P, BANK], F32, tag="flip")
+            for u in range(2):
+                nc.tensor.transpose(
+                    bank[:, P * u : P * (u + 1)], x_sb[:].bitcast(F32)[:, P * u : P * (u + 1)], ident[:]
+                )
+            nc.vector.tensor_copy(
+                out=x_grouped[:].bitcast(F32).rearrange("w (t u) -> w t u", u=2),
+                in_=bank[:, 0 : 2 * P].rearrange("w (u t) -> w t u", u=2),
             )
-        nc.vector.tensor_copy(
-            out=x_grouped[:].bitcast(F32).rearrange("w (t u) -> w t u", u=2),
-            in_=bank[:, 0 : 2 * P].rearrange("w (u t) -> w t u", u=2),
-        )
-        nc.vector.quantize_mx(out=x_codes[:].bitcast(FP8X4), scales=x_scales[:], in_=x_grouped[:])
+            nc.vector.quantize_mx(out=x_codes[:].bitcast(FP8X4), scales=x_scales[:], in_=x_grouped[:])
 
         wi_grouped = keep.tile([P, COLS * 4], BF16, align_bytes=64)
         wi_codes = keep.tile([P, COLS], U32, align_bytes=64)
@@ -220,27 +228,31 @@ def tile_mamba3core_s_kernel(
                     stop=True,
                 )
 
-        def states(which, g):
+        def copy_xi(g):
             h, half = divmod(g, 2)
+            cols = slice(GROUP_COLS * g, GROUP_COLS * (g + 1))
+            nc.scalar.copy(
+                out=xi_sb[:, cols].rearrange("t (p e) -> t p e", e=2),
+                in_=xi_by_token[h][:, half, :].rearrange("t (e p) -> t p e", e=2),
+            )
+
+        def states(which, g, engine, b_all):
             flat = slice(GROUP_FLAT * g, GROUP_FLAT * (g + 1))
-            in_order = xi_by_token[h][:, half, :].rearrange("t (e p) -> t p e", e=2)
-            if which == "i" and g < GPSIMD_GROUPS:
-                cols = slice(GROUP_COLS * g, GROUP_COLS * (g + 1))
-                nc.scalar.copy(out=xi_sb[:, cols].rearrange("t (p e) -> t p e", e=2), in_=in_order)
-                nc.gpsimd.tensor_tensor(
-                    out=state_sb[which][:, flat].rearrange("t (c n) -> t c n", n=STATES),
-                    in0=xi_sb[:, cols].unsqueeze(2).to_broadcast([P, GROUP_COLS, STATES]),
-                    in1=spread[which][:, flat].rearrange("t (c n) -> t c n", n=STATES),
-                    op=ALU.mult,
-                )
-            else:
-                nc.vector.tensor_tensor(
-                    out=state_sb[which][:, flat].rearrange("t (p e n) -> t p e n", e=2, n=STATES),
-                    in0=in_order.unsqueeze(3).to_broadcast([P, P, 2, STATES]),
-                    in1=spread[which][:, flat].rearrange("t (p e n) -> t p e n", e=2, n=STATES),
-                    op=ALU.mult,
-                )
+            cols = slice(GROUP_COLS * g, GROUP_COLS * (g + 1))
+            engine.tensor_tensor(
+                out=state_sb[which][:, flat].rearrange("t (c n) -> t c n", n=STATES),
+                in0=xi_sb[:, cols].unsqueeze(2).to_broadcast([P, GROUP_COLS, STATES]),
+                in1=b_all.rearrange("t (c n) -> t c n", n=STATES),
+                op=ALU.mult,
+            )
             nc.sync.dma_start(out=state_rows[which][:, flat], in_=state_sb[which][:, flat])
+
+        def states_imag(g):
+            states("i", g, nc.gpsimd, b_imag_all[:, GROUP_FLAT * g : GROUP_FLAT * (g + 1)])
+
+        def states_real(g):
+            bank = spread_row(g, 3)
+            states("r", g, nc.vector, bank[:, 0:GROUP_WORDS].bitcast(BF16))
 
         def make_y(h):
             nc.vector.tensor_tensor(
@@ -254,60 +266,77 @@ def tile_mamba3core_s_kernel(
         wo_codes = keep.tile([P, PASSES, D], U32, align_bytes=64)
         wo_scales = keep.tile([P, PASSES, D], U8, align_bytes=64)
 
-        def flip_w_out(pair):
-            for h in range(PASSES):
-                bank = flips.tile([P, BANK], F32, tag="flip")
-                for il in range(2):
-                    for a in range(2):
-                        first = 256 * h + P * a
-                        nc.tensor.transpose(
-                            bank[:, P * (2 * il + a) : P * (2 * il + a + 1)],
-                            wo_sb[:, 2 * pair + il, :].bitcast(F32)[:, first : first + P],
-                            ident[:],
-                        )
-                nc.scalar.copy(
-                    out=wo_grouped[:, h, :].bitcast(F32)[:, BANK * pair : BANK * (pair + 1)].rearrange(
-                        "p (il q a) -> p il q a", il=2, a=2
-                    ),
-                    in_=bank[:].rearrange("p (il a q) -> p il q a", il=2, a=2),
-                )
+        def flip_w_out(pair, h):
+            rows = slice(256 * pair, 256 * (pair + 1))
+            bank = flips.tile([P, BANK], F32, tag="flip")
+            for il in range(2):
+                for a in range(2):
+                    first = 256 * h + P * a
+                    nc.tensor.transpose(
+                        bank[:, P * (2 * il + a) : P * (2 * il + a + 1)],
+                        wo_sb[:, 2 * pair + il, :].bitcast(F32)[:, first : first + P],
+                        ident[:],
+                    )
+            nc.scalar.copy(
+                out=wo_grouped[:, h, :].bitcast(F32)[:, BANK * pair : BANK * (pair + 1)].rearrange(
+                    "p (il q a) -> p il q a", il=2, a=2
+                ),
+                in_=bank[:].rearrange("p (il a q) -> p il q a", il=2, a=2),
+            )
+            nc.vector.quantize_mx(
+                out=wo_codes[:, h, rows].bitcast(FP8X4),
+                scales=wo_scales[:, h, rows],
+                in_=wo_grouped[:, h, 4 * 256 * pair : 4 * 256 * (pair + 1)],
+            )
 
-        flip_w_in(0)
-        first_matmul(0)
-        states("r", 0)
-        states("i", 0)
-        spread_group(1)
-        flip_w_in(1)
-        first_matmul(1)
-        make_y(0)
-        states("r", 1)
-        states("i", 1)
-        spread_group(2)
-        flip_w_in(2)
-        first_matmul(2)
-        states("r", 2)
-        states("i", 2)
-        spread_group(3)
-        flip_w_in(3)
-        first_matmul(3)
-        make_y(1)
         y_codes = keep.tile([P, PASSES * P], U32, align_bytes=64)
         y_scales = keep.tile([P, PASSES * P], U8, align_bytes=64)
+
+        turn_for_spreading()
+        spread_b_imag(0)
+        flip_x()
+        flip_w_in(0)
+        flip_w_in(1)
+        make_gain()
+
+        first_matmul(0)
+        copy_xi(0)
+        states_imag(0)
+        states_real(0)
+        flip_w_in(2)
+        spread_b_imag(1)
+
+        first_matmul(1)
+        copy_xi(1)
+        states_imag(1)
+        states_real(1)
+        make_y(0)
+        flip_w_in(3)
+        spread_b_imag(2)
+
+        first_matmul(2)
+        copy_xi(2)
+        states_imag(2)
+        states_real(2)
+        flip_w_out(0, 0)
+        flip_w_out(0, 1)
+        spread_b_imag(3)
+
+        first_matmul(3)
+        copy_xi(3)
+        states_imag(3)
+        make_y(1)
         nc.vector.quantize_mx(
             out=y_codes[:].bitcast(FP8X4),
             scales=y_scales[:],
             in_=y_grouped[:].rearrange("p h t j -> p (h t j)"),
         )
-        flip_w_out(0)
-        flip_w_out(1)
-        spread_row("w", NORM_ROW, 0, 2)
-        for h in range(PASSES):
-            nc.vector.quantize_mx(
-                out=wo_codes[:, h, :].bitcast(FP8X4), scales=wo_scales[:, h, :], in_=wo_grouped[:, h, :]
-            )
-        states("r", 3)
+        flip_w_out(1, 0)
+        flip_w_out(1, 1)
+        states_real(3)
+        spread_norm_w()
 
-        acc = out_acc.tile([P, D], F32)
+        acc = xi_col.tile([P, D], F32, tag="xi_col")
         for h in range(PASSES):
             nc.tensor.matmul_mx(
                 out=acc[:],
@@ -324,13 +353,12 @@ def tile_mamba3core_s_kernel(
         nc.scalar.activation(out=squares[:], in_=acc[:], func=ACT.Square, accum_out=sum_sq[:])
         rms = keep.tile([P, 1], F32)
         nc.scalar.activation(out=rms[:], in_=sum_sq[:], func=ACT.Sqrt, bias=eps[:], scale=1.0 / D)
+        weighted = keep.tile([P, D], F32)
+        nc.vector.tensor_tensor(out=weighted[:], in0=acc[:], in1=norm_w_all[:], op=ALU.mult)
         inv_rms = keep.tile([P, 1], F32)
         nc.vector.reciprocal(out=inv_rms[:], in_=rms[:])
         res = keep.tile([P, D], F32)
         nc.vector.scalar_tensor_tensor(
-            out=res[:], in0=acc[:], scalar=inv_rms[:], in1=spread["w"][:], op0=ALU.mult, op1=ALU.mult
+            out=res[:], in0=weighted[:], scalar=inv_rms[:], in1=x_sb[:], op0=ALU.mult, op1=ALU.add
         )
-        nc.vector.tensor_tensor(out=res[:], in0=res[:], in1=x_sb[:], op=ALU.add)
         nc.sync.dma_start(out=res_rows, in_=res[:])
-
-        states("i", 3)

@@ -53,6 +53,22 @@ def tile_mamba3core_s_kernel(
         eps = keep.tile([P, 1], F32)
         nc.vector.memset(eps[:], EPS)
 
+        zeros = keep.tile([P, BANK], F32)
+        nc.vector.memset(zeros[:], 0.0)
+        idle_bank = flips.tile([P, BANK], F32, tag="flip")
+        nc.tensor.matmul(out=idle_bank[:], lhsT=zeros[:, 0:P], rhs=zeros[:], start=True, stop=True)
+
+        x_sb = keep.tile([P, D], BF16)
+        nc.sync.dma_start(out=x_sb[:], in_=x_rows)
+        wi_sb = keep.tile([P, GROUPS, 2 * D], BF16)
+
+        def load_w_in(g):
+            nc.sync.dma_start(
+                out=wi_sb[:, g, :],
+                in_=W_in[GROUP_COLS * g : GROUP_COLS * (g + 1), :].rearrange("(p e) k -> p (e k)", e=2),
+            )
+
+        load_w_in(0)
         for v, src in enumerate((B_real, B_imag, C_real, C_imag)):
             nc.sync.dma_start(
                 out=vec_rows[GROUPS * v : GROUPS * (v + 1), :],
@@ -61,14 +77,8 @@ def tile_mamba3core_s_kernel(
         nc.sync.dma_start(
             out=vec_rows[NORM_ROW : NORM_ROW + 1, 0:D], in_=norm_w.rearrange("(o d) -> o d", o=1)
         )
-        x_sb = keep.tile([P, D], BF16)
-        nc.sync.dma_start(out=x_sb[:], in_=x_rows)
-        wi_sb = keep.tile([P, GROUPS, 2 * D], BF16)
-        for g in range(GROUPS):
-            nc.sync.dma_start(
-                out=wi_sb[:, g, :],
-                in_=W_in[GROUP_COLS * g : GROUP_COLS * (g + 1), :].rearrange("(p e) k -> p (e k)", e=2),
-            )
+        for g in range(1, GROUPS):
+            load_w_in(g)
         wo_sb = keep.tile([P, 4, COLS], BF16)
         for pair in range(2):
             nc.sync.dma_start(
@@ -292,10 +302,10 @@ def tile_mamba3core_s_kernel(
         y_codes = keep.tile([P, PASSES * P], U32, align_bytes=64)
         y_scales = keep.tile([P, PASSES * P], U8, align_bytes=64)
 
-        turn_for_spreading()
-        spread_b_imag(0)
         flip_x()
         flip_w_in(0)
+        turn_for_spreading()
+        spread_b_imag(0)
         flip_w_in(1)
         make_gain()
 

@@ -24,6 +24,7 @@ FLAT = GROUPS * GROUP_FLAT
 BANK = 512
 NORM_ROW = 4 * GROUPS
 EPS = 2.0 ** -23
+IDLE_PASSES = 4
 
 FLOPS = 2 * (2 * P * D * COLS)
 
@@ -238,6 +239,20 @@ def tile_mamba3core_s_kernel(
                     stop=True,
                 )
 
+        def idle_passes(g):
+            cols = slice(GROUP_COLS * g, GROUP_COLS * (g + 1))
+            bank = flips.tile([P, BANK], F32, tag="flip")
+            for i in range(IDLE_PASSES):
+                nc.tensor.matmul_mx(
+                    out=bank[:, 0:GROUP_COLS],
+                    lhsT=x_codes[:].bitcast(FP8X4),
+                    lhsT_scale=x_scales[:],
+                    rhs=wi_codes[:, cols].bitcast(FP8X4),
+                    rhs_scale=wi_scales[:, cols],
+                    start=True,
+                    stop=True,
+                )
+
         def copy_xi(g):
             h, half = divmod(g, 2)
             cols = slice(GROUP_COLS * g, GROUP_COLS * (g + 1))
@@ -310,6 +325,7 @@ def tile_mamba3core_s_kernel(
         make_gain()
 
         first_matmul(0)
+        idle_passes(0)
         copy_xi(0)
         states_imag(0)
         states_real(0)
@@ -317,6 +333,7 @@ def tile_mamba3core_s_kernel(
         spread_b_imag(1)
 
         first_matmul(1)
+        idle_passes(1)
         copy_xi(1)
         states_imag(1)
         states_real(1)
@@ -325,6 +342,7 @@ def tile_mamba3core_s_kernel(
         spread_b_imag(2)
 
         first_matmul(2)
+        idle_passes(2)
         copy_xi(2)
         states_imag(2)
         states_real(2)
@@ -333,6 +351,7 @@ def tile_mamba3core_s_kernel(
         spread_b_imag(3)
 
         first_matmul(3)
+        idle_passes(3)
         copy_xi(3)
         states_imag(3)
         make_y(1)

@@ -24,7 +24,6 @@ FLAT = GROUPS * GROUP_FLAT
 BANK = 512
 NORM_ROW = 4 * GROUPS
 EPS = 2.0 ** -23
-IDLE_PASSES = 4
 
 FLOPS = 2 * (2 * P * D * COLS)
 
@@ -42,8 +41,9 @@ def tile_mamba3core_s_kernel(
 
     with ExitStack() as ctx:
         keep = ctx.enter_context(tc.tile_pool(name="keep", bufs=1))
-        flips = ctx.enter_context(tc.psum_pool(name="flips", bufs=4))
-        xi_tok = ctx.enter_context(tc.psum_pool(name="xi_tok", bufs=2))
+        flips = ctx.enter_context(tc.psum_pool(name="flips", bufs=3))
+        spreads = ctx.enter_context(tc.psum_pool(name="spreads", bufs=2))
+        xi_tok = ctx.enter_context(tc.psum_pool(name="xi_tok", bufs=1))
         xi_col = ctx.enter_context(tc.psum_pool(name="xi_col", bufs=2))
         ctx.enter_context(tc.manual_schedule())
 
@@ -53,11 +53,6 @@ def tile_mamba3core_s_kernel(
         make_identity(nc, ident[:])
         eps = keep.tile([P, 1], F32)
         nc.vector.memset(eps[:], EPS)
-
-        zeros = keep.tile([P, BANK], F32)
-        nc.vector.memset(zeros[:], 0.0)
-        idle_bank = flips.tile([P, BANK], F32, tag="flip")
-        nc.tensor.matmul(out=idle_bank[:], lhsT=zeros[:, 0:P], rhs=zeros[:], start=True, stop=True)
 
         x_sb = keep.tile([P, D], BF16)
         nc.sync.dma_start(out=x_sb[:], in_=x_rows)
@@ -135,8 +130,8 @@ def tile_mamba3core_s_kernel(
                 out=gain[:].rearrange("p h j -> p (h j)"), in_=rr[:], axis=mybir.AxisListType.X, op=ALU.add
             )
 
-        def spread_row(row, slices):
-            bank = flips.tile([P, BANK], F32, tag="flip")
+        def spread_row(pool, row, slices):
+            bank = pool.tile([P, BANK], F32, tag="flip")
             for s in range(slices):
                 nc.tensor.transpose(
                     bank[:, P * s : P * (s + 1)],
@@ -149,14 +144,14 @@ def tile_mamba3core_s_kernel(
         norm_w_all = keep.tile([P, D], BF16)
 
         def spread_b_imag(g):
-            bank = spread_row(GROUPS + g, 3)
+            bank = spread_row(flips, GROUPS + g, 3)
             nc.scalar.copy(
                 out=b_imag_all[:].bitcast(F32)[:, GROUP_WORDS * g : GROUP_WORDS * (g + 1)],
                 in_=bank[:, 0:GROUP_WORDS],
             )
 
         def spread_norm_w():
-            bank = spread_row(NORM_ROW, 2)
+            bank = spread_row(flips, NORM_ROW, 2)
             nc.scalar.copy(out=norm_w_all[:].bitcast(F32), in_=bank[:, 0 : D // 2])
 
         x_grouped = keep.tile([P, P * 4], BF16, align_bytes=64)
@@ -239,20 +234,6 @@ def tile_mamba3core_s_kernel(
                     stop=True,
                 )
 
-        def idle_passes(g):
-            cols = slice(GROUP_COLS * g, GROUP_COLS * (g + 1))
-            bank = flips.tile([P, BANK], F32, tag="flip")
-            for i in range(IDLE_PASSES):
-                nc.tensor.matmul_mx(
-                    out=bank[:, 0:GROUP_COLS],
-                    lhsT=x_codes[:].bitcast(FP8X4),
-                    lhsT_scale=x_scales[:],
-                    rhs=wi_codes[:, cols].bitcast(FP8X4),
-                    rhs_scale=wi_scales[:, cols],
-                    start=True,
-                    stop=True,
-                )
-
         def copy_xi(g):
             h, half = divmod(g, 2)
             cols = slice(GROUP_COLS * g, GROUP_COLS * (g + 1))
@@ -276,7 +257,7 @@ def tile_mamba3core_s_kernel(
             states("i", g, nc.gpsimd, b_imag_all[:, GROUP_FLAT * g : GROUP_FLAT * (g + 1)])
 
         def states_real(g):
-            bank = spread_row(g, 3)
+            bank = spread_row(spreads, g, 3)
             states("r", g, nc.vector, bank[:, 0:GROUP_WORDS].bitcast(BF16))
 
         def make_y(h):
@@ -320,38 +301,33 @@ def tile_mamba3core_s_kernel(
         flip_x()
         flip_w_in(0)
         turn_for_spreading()
-        spread_b_imag(0)
         flip_w_in(1)
-        make_gain()
+        spread_b_imag(0)
 
         first_matmul(0)
-        idle_passes(0)
         copy_xi(0)
         states_imag(0)
         states_real(0)
         flip_w_in(2)
         spread_b_imag(1)
+        make_gain()
 
         first_matmul(1)
-        idle_passes(1)
         copy_xi(1)
         states_imag(1)
         states_real(1)
-        make_y(0)
         flip_w_in(3)
+        make_y(0)
         spread_b_imag(2)
 
         first_matmul(2)
-        idle_passes(2)
         copy_xi(2)
         states_imag(2)
         states_real(2)
-        flip_w_out(0, 0)
-        flip_w_out(0, 1)
         spread_b_imag(3)
+        flip_w_out(0, 0)
 
         first_matmul(3)
-        idle_passes(3)
         copy_xi(3)
         states_imag(3)
         make_y(1)
@@ -360,6 +336,7 @@ def tile_mamba3core_s_kernel(
             scales=y_scales[:],
             in_=y_grouped[:].rearrange("p h t j -> p (h t j)"),
         )
+        flip_w_out(0, 1)
         flip_w_out(1, 0)
         flip_w_out(1, 1)
         states_real(3)

from contextlib import ExitStack

from concourse import mybir
from concourse.masks import make_identity

F32 = mybir.dt.float32
BF16 = mybir.dt.bfloat16
U32 = mybir.dt.uint32
U8 = mybir.dt.uint8
FP8X4 = mybir.dt.float8_e4m3fn_x4
ALU = mybir.AluOpType
ACT = mybir.ActivationFunctionType

P = 128
D = 512
PASSES = 2
GROUPS = 4
GROUP_COLS = 2 * P
STATES = 3
COLS = GROUPS * GROUP_COLS
GROUP_FLAT = GROUP_COLS * STATES
GROUP_WORDS = GROUP_FLAT // 2
FLAT = GROUPS * GROUP_FLAT
BANK = 512
NORM_ROW = 4 * GROUPS
EPS = 2.0 ** -23

FLOPS = 2 * (2 * P * D * COLS)


def tile_mamba3core_s_kernel(
    tc, x, W_in, W_out, A_theta, B_real, B_imag, C_real, C_imag, norm_w, out_0, out_1, out_2
):
    nc = tc.nc
    x_rows = x.flatten_outer_dims()
    res_rows = out_0.flatten_outer_dims()
    state_rows = {
        "r": out_1.rearrange("b l c d n -> (b l) (c d n)"),
        "i": out_2.rearrange("b l c d n -> (b l) (c d n)"),
    }

    with ExitStack() as ctx:
        keep = ctx.enter_context(tc.tile_pool(name="keep", bufs=1))
        flips = ctx.enter_context(tc.psum_pool(name="flips", bufs=3))
        spreads = ctx.enter_context(tc.psum_pool(name="spreads", bufs=2))
        xi_tok = ctx.enter_context(tc.psum_pool(name="xi_tok", bufs=1))
        xi_col = ctx.enter_context(tc.psum_pool(name="xi_col", bufs=2))
        ctx.enter_context(tc.manual_schedule())

        vec_rows = keep.tile([P, GROUP_FLAT], BF16)
        nc.gpsimd.memset(vec_rows[:].bitcast(F32), 0.0)
        ident = keep.tile([P, P], F32)
        make_identity(nc, ident[:])
        eps = keep.tile([P, 1], F32)
        nc.vector.memset(eps[:], EPS)

        x_sb = keep.tile([P, D], BF16)
        nc.sync.dma_start(out=x_sb[:], in_=x_rows)
        wi_sb = keep.tile([P, GROUPS, 2 * D], BF16)

        def load_w_in(g):
            nc.sync.dma_start(
                out=wi_sb[:, g, :],
                in_=W_in[GROUP_COLS * g : GROUP_COLS * (g + 1), :].rearrange("(p e) k -> p (e k)", e=2),
            )

        load_w_in(0)
        for v, src in enumerate((B_real, B_imag, C_real, C_imag)):
            nc.sync.dma_start(
                out=vec_rows[GROUPS * v : GROUPS * (v + 1), :],
                in_=src.rearrange("a d n -> (a d n)").rearrange("(g f) -> g f", f=GROUP_FLAT),
            )
        nc.sync.dma_start(
            out=vec_rows[NORM_ROW : NORM_ROW + 1, 0:D], in_=norm_w.rearrange("(o d) -> o d", o=1)
        )
        for g in range(1, GROUPS):
            load_w_in(g)
        wo_sb = keep.tile([P, 4, COLS], BF16)
        for pair in range(2):
            nc.sync.dma_start(
                out=wo_sb[:, 2 * pair : 2 * pair + 2, :],
                in_=W_out[256 * pair : 256 * (pair + 1), :].rearrange("(i q) k -> q i k", q=P),
            )
        warm = keep.tile([P, 1], F32)
        nc.scalar.activation(out=warm[:], in_=eps[:], func=ACT.Sqrt)

        vec_words = vec_rows[:].bitcast(F32)
        vec_cols = keep.tile([P, 3, 32], F32)
        own_words = keep.tile([P, 4 * GROUPS, 3], F32)
        rr = keep.tile([P, GROUPS * 2, STATES], F32)
        ii = keep.tile([P, GROUPS * 2, STATES], F32)
        gain = keep.tile([P, PASSES, 4], F32)

        def turn_for_spreading():
            bank = flips.tile([P, BANK], F32, tag="flip")
            for s in range(3):
                nc.tensor.transpose(
                    bank[:, P * s : P * (s + 1)], vec_words[:, P * s : P * (s + 1)], ident[:]
                )
            nc.scalar.copy(
                out=vec_cols[:], in_=bank[:, 0 : 3 * P].rearrange("w (s r) -> w s r", s=3)[:, :, 0:32]
            )

        def make_gain():
            bank = flips.tile([P, BANK], F32, tag="flip")
            for s in range(3):
                nc.tensor.transpose(
                    bank[:, P * s : P * (s + 1)], vec_words[:, s : GROUP_WORDS : 3], ident[:]
                )
            nc.vector.tensor_copy(
                out=own_words[:],
                in_=bank[:, 0 : 3 * P].rearrange("p (s r) -> p r s", s=3)[:, 0 : 4 * GROUPS, :],
            )
            own = own_words[:].rearrange("p r s -> p (r s)").bitcast(BF16)
            per_vec = GROUPS * 2 * STATES
            nc.vector.tensor_tensor(
                out=rr[:].rearrange("p a n -> p (a n)"),
                in0=own[:, 2 * per_vec : 3 * per_vec],
                in1=own[:, 0:per_vec],
                op=ALU.mult,
            )
            nc.vector.tensor_tensor(
                out=ii[:].rearrange("p a n -> p (a n)"),
                in0=own[:, 3 * per_vec : 4 * per_vec],
                in1=own[:, per_vec : 2 * per_vec],
                op=ALU.mult,
            )
            nc.vector.tensor_tensor(out=rr[:], in0=rr[:], in1=ii[:], op=ALU.subtract)
            nc.vector.tensor_reduce(
                out=gain[:].rearrange("p h j -> p (h j)"), in_=rr[:], axis=mybir.AxisListType.X, op=ALU.add
            )

        def spread_row(pool, row, slices):
            bank = pool.tile([P, BANK], F32, tag="flip")
            for s in range(slices):
                nc.tensor.transpose(
                    bank[:, P * s : P * (s + 1)],
                    vec_cols[:, s, row : row + 1].to_broadcast([P, P]),
                    ident[:],
                )
            return bank

        b_imag_all = keep.tile([P, FLAT], BF16)
        norm_w_all = keep.tile([P, D], BF16)

        def spread_b_imag(g):
            bank = spread_row(flips, GROUPS + g, 3)
            nc.scalar.copy(
                out=b_imag_all[:].bitcast(F32)[:, GROUP_WORDS * g : GROUP_WORDS * (g + 1)],
                in_=bank[:, 0:GROUP_WORDS],
            )

        def spread_norm_w():
            bank = spread_row(flips, NORM_ROW, 2)
            nc.scalar.copy(out=norm_w_all[:].bitcast(F32), in_=bank[:, 0 : D // 2])

        x_grouped = keep.tile([P, P * 4], BF16, align_bytes=64)
        x_codes = keep.tile([P, P], U32, align_bytes=64)
        x_scales = keep.tile([P, P], U8, align_bytes=64)

        def flip_x():
            bank = flips.tile([P, BANK], F32, tag="flip")
            for u in range(2):
                nc.tensor.transpose(
                    bank[:, P * u : P * (u + 1)], x_sb[:].bitcast(F32)[:, P * u : P * (u + 1)], ident[:]
                )
            nc.vector.tensor_copy(
                out=x_grouped[:].bitcast(F32).rearrange("w (t u) -> w t u", u=2),
                in_=bank[:, 0 : 2 * P].rearrange("w (u t) -> w t u", u=2),
            )
            nc.vector.quantize_mx(out=x_codes[:].bitcast(FP8X4), scales=x_scales[:], in_=x_grouped[:])

        wi_grouped = keep.tile([P, COLS * 4], BF16, align_bytes=64)
        wi_codes = keep.tile([P, COLS], U32, align_bytes=64)
        wi_scales = keep.tile([P, COLS], U8, align_bytes=64)

        def flip_w_in(g):
            cols = slice(GROUP_COLS * g, GROUP_COLS * (g + 1))
            bank = flips.tile([P, BANK], F32, tag="flip")
            for e in range(2):
                for u in range(2):
                    first = 256 * e + P * u
                    nc.tensor.transpose(
                        bank[:, P * (2 * e + u) : P * (2 * e + u + 1)],
                        wi_sb[:, g, :].bitcast(F32)[:, first : first + P],
                        ident[:],
                    )
            copy = nc.vector.tensor_copy if g == 0 else nc.scalar.copy
            copy(
                out=wi_grouped[:].bitcast(F32)[:, BANK * g : BANK * (g + 1)].rearrange(
                    "w (e p u) -> w e p u", e=2, u=2
                ),
                in_=bank[:].rearrange("w (e u p) -> w e p u", e=2, u=2),
            )
            nc.vector.quantize_mx(
                out=wi_codes[:, cols].bitcast(FP8X4),
                scales=wi_scales[:, cols],
                in_=wi_grouped[:, 4 * GROUP_COLS * g : 4 * GROUP_COLS * (g + 1)],
            )

        state_sb = {
            "r": keep.tile([P, FLAT], F32, name="state_r"),
            "i": keep.tile([P, FLAT], F32, name="state_i"),
        }
        xi_sb = keep.tile([P, COLS], F32)
        y_grouped = keep.tile([P, PASSES, P, 4], BF16, align_bytes=64)
        xi_by_token = {}
        xi_by_column = {}

        def first_matmul(g):
            h, half = divmod(g, 2)
            cols = slice(GROUP_COLS * g, GROUP_COLS * (g + 1))
            if half == 0:
                xi_by_token[h] = xi_tok.tile([P, 2, GROUP_COLS], F32, name="xi_by_token", tag="xi_tok")
                xi_by_column[h] = xi_col.tile([P, 4, P], F32, name="xi_by_column", tag="xi_col")
            nc.tensor.matmul_mx(
                out=xi_by_token[h][:, half, :],
                lhsT=x_codes[:].bitcast(FP8X4),
                lhsT_scale=x_scales[:],
                rhs=wi_codes[:, cols].bitcast(FP8X4),
                rhs_scale=wi_scales[:, cols],
                start=True,
                stop=True,
            )
            for e in range(2):
                part = slice(GROUP_COLS * g + P * e, GROUP_COLS * g + P * (e + 1))
                nc.tensor.matmul_mx(
                    out=xi_by_column[h][:, 2 * half + e, :],
                    lhsT=wi_codes[:, part].bitcast(FP8X4),
                    lhsT_scale=wi_scales[:, part],
                    rhs=x_codes[:].bitcast(FP8X4),
                    rhs_scale=x_scales[:],
                    start=True,
                    stop=True,
                )

        def copy_xi(g):
            h, half = divmod(g, 2)
            cols = slice(GROUP_COLS * g, GROUP_COLS * (g + 1))
            nc.scalar.copy(
                out=xi_sb[:, cols].rearrange("t (p e) -> t p e", e=2),
                in_=xi_by_token[h][:, half, :].rearrange("t (e p) -> t p e", e=2),
            )

        def states(which, g, engine, b_all):
            flat = slice(GROUP_FLAT * g, GROUP_FLAT * (g + 1))
            cols = slice(GROUP_COLS * g, GROUP_COLS * (g + 1))
            engine.tensor_tensor(
                out=state_sb[which][:, flat].rearrange("t (c n) -> t c n", n=STATES),
                in0=xi_sb[:, cols].unsqueeze(2).to_broadcast([P, GROUP_COLS, STATES]),
                in1=b_all.rearrange("t (c n) -> t c n", n=STATES),
                op=ALU.mult,
            )
            nc.sync.dma_start(out=state_rows[which][:, flat], in_=state_sb[which][:, flat])

        def states_imag(g):
            states("i", g, nc.gpsimd, b_imag_all[:, GROUP_FLAT * g : GROUP_FLAT * (g + 1)])

        def states_real(g):
            bank = spread_row(spreads, g, 3)
            states("r", g, nc.vector, bank[:, 0:GROUP_WORDS].bitcast(BF16))

        def make_y(h):
            nc.vector.tensor_tensor(
                out=y_grouped[:, h, :, :],
                in0=xi_by_column[h][:].rearrange("p j t -> p t j"),
                in1=gain[:, h, :].unsqueeze(1).to_broadcast([P, P, 4]),
                op=ALU.mult,
            )

        wo_grouped = keep.tile([P, PASSES, D * 4], BF16, align_bytes=64)
        wo_codes = keep.tile([P, PASSES, D], U32, align_bytes=64)
        wo_scales = keep.tile([P, PASSES, D], U8, align_bytes=64)

        def flip_w_out(pair, h):
            rows = slice(256 * pair, 256 * (pair + 1))
            bank = flips.tile([P, BANK], F32, tag="flip")
            for il in range(2):
                for a in range(2):
                    first = 256 * h + P * a
                    nc.tensor.transpose(
                        bank[:, P * (2 * il + a) : P * (2 * il + a + 1)],
                        wo_sb[:, 2 * pair + il, :].bitcast(F32)[:, first : first + P],
                        ident[:],
                    )
            nc.scalar.copy(
                out=wo_grouped[:, h, :].bitcast(F32)[:, BANK * pair : BANK * (pair + 1)].rearrange(
                    "p (il q a) -> p il q a", il=2, a=2
                ),
                in_=bank[:].rearrange("p (il a q) -> p il q a", il=2, a=2),
            )
            nc.vector.quantize_mx(
                out=wo_codes[:, h, rows].bitcast(FP8X4),
                scales=wo_scales[:, h, rows],
                in_=wo_grouped[:, h, 4 * 256 * pair : 4 * 256 * (pair + 1)],
            )

        y_codes = keep.tile([P, PASSES * P], U32, align_bytes=64)
        y_scales = keep.tile([P, PASSES * P], U8, align_bytes=64)

        flip_x()
        flip_w_in(0)
        turn_for_spreading()
        flip_w_in(1)
        spread_b_imag(0)

        first_matmul(0)
        copy_xi(0)
        states_imag(0)
        states_real(0)
        flip_w_in(2)
        spread_b_imag(1)
        make_gain()

        first_matmul(1)
        copy_xi(1)
        states_imag(1)
        states_real(1)
        flip_w_in(3)
        make_y(0)
        spread_b_imag(2)

        first_matmul(2)
        copy_xi(2)
        states_imag(2)
        states_real(2)
        spread_b_imag(3)
        flip_w_out(0, 0)

        first_matmul(3)
        copy_xi(3)
        states_imag(3)
        make_y(1)
        nc.vector.quantize_mx(
            out=y_codes[:].bitcast(FP8X4),
            scales=y_scales[:],
            in_=y_grouped[:].rearrange("p h t j -> p (h t j)"),
        )
        flip_w_out(0, 1)
        flip_w_out(1, 0)
        flip_w_out(1, 1)
        states_real(3)
        spread_norm_w()

        acc = xi_col.tile([P, D], F32, tag="xi_col")
        for h in range(PASSES):
            nc.tensor.matmul_mx(
                out=acc[:],
                lhsT=y_codes[:, P * h : P * (h + 1)].bitcast(FP8X4),
                lhsT_scale=y_scales[:, P * h : P * (h + 1)],
                rhs=wo_codes[:, h, :].bitcast(FP8X4),
                rhs_scale=wo_scales[:, h, :],
                start=(h == 0),
                stop=(h == PASSES - 1),
            )

        squares = keep.tile([P, D], F32)
        sum_sq = keep.tile([P, 1], F32)
        nc.scalar.activation(out=squares[:], in_=acc[:], func=ACT.Square, accum_out=sum_sq[:])
        rms = keep.tile([P, 1], F32)
        nc.scalar.activation(out=rms[:], in_=sum_sq[:], func=ACT.Sqrt, bias=eps[:], scale=1.0 / D)
        weighted = keep.tile([P, D], F32)
        nc.vector.tensor_tensor(out=weighted[:], in0=acc[:], in1=norm_w_all[:], op=ALU.mult)
        inv_rms = keep.tile([P, 1], F32)
        nc.vector.reciprocal(out=inv_rms[:], in_=rms[:])
        res = keep.tile([P, D], F32)
        nc.vector.scalar_tensor_tensor(
            out=res[:], in0=weighted[:], scalar=inv_rms[:], in1=x_sb[:], op0=ALU.mult, op1=ALU.add
        )
        nc.sync.dma_start(out=res_rows, in_=res[:])
